import numpy as np
import ml_dtypes


def mxq(x, axis, fmt="e4m3"):
    dtype, down = {"e4m3": (ml_dtypes.float8_e4m3fn, 7), "e5m2": (ml_dtypes.float8_e5m2, 14)}[fmt]
    v = np.moveaxis(np.asarray(x, np.float32).astype(ml_dtypes.bfloat16).astype(np.float64), axis, -1)
    blocks = v.reshape(v.shape[:-1] + (-1, 32))
    amax = np.abs(blocks).max(-1, keepdims=True)
    byte = np.maximum(np.where(amax > 0, np.frexp(amax)[1] - 1 + 127, 0) - down, 1)
    scale = np.exp2(byte - 127.0)
    codes = (blocks / scale).astype(np.float32).astype(dtype).astype(np.float64)
    return np.moveaxis((codes * scale).reshape(v.shape), -1, axis)


WIDE = False


def mx_kscale(k):
    if not WIDE:
        return np.ones(k)
    levels = np.array([10, -10, 5, -5, 0])
    if k % 512:
        return np.exp2(np.random.permutation(np.resize(levels, k // 32))).repeat(32)
    a = np.empty((k // 512, 16))
    for p in range(k // 512):
        a[p, :8] = np.random.permutation(np.resize(levels, 8))
        for g in range(8):
            far = levels[np.abs(levels - a[p, g]) >= 10]
            a[p, g + 8] = far[np.random.randint(len(far))]
    return np.exp2(a.ravel()).repeat(32)


BF16 = ml_dtypes.bfloat16


def bf(x):
    return np.asarray(x, np.float32).astype(BF16)


def f64(x):
    return np.asarray(x).astype(np.float64)


B, T, G, I, H = 4, 256, 8, 512, 512


def setup_inputs():
    s = mx_kscale(I)
    return {"x": bf((np.random.standard_normal((B, T, G, I)) * s).reshape(B, T, G * I)),
            "W": bf(np.random.standard_normal((G, H, I)) / np.sqrt(I) / s),
            "b": bf(np.random.standard_normal((G, H)) * 0.5)}


def core(x, W, b):
    xg = f64(x).reshape(B, T, G, I)
    xq = mxq(xg, 3, "e4m3")
    wq = mxq(f64(W), 2, "e4m3")
    y = xq.transpose(2, 0, 1, 3).reshape(G, B * T, I) @ wq.transpose(0, 2, 1)
    out = y.reshape(G, B, T, H).transpose(1, 2, 0, 3) + f64(b)
    return np.swapaxes(out, -1, -2).reshape(B, T, G * H)


def e4m3fn_bytes(y):
    return np.clip(np.asarray(y, np.float64), -448.0, 448.0).astype(np.float32).astype(ml_dtypes.float8_e4m3fn).view(np.uint8)


Y_SCALE = 200.0


def reference(x, W, b):
    out = core(x, W, b)
    return out, e4m3fn_bytes(out * Y_SCALE)

@@ -1,0 +1,256 @@
+from contextlib import ExitStack
+
+import concourse.mybir as mybir
+from concourse.masks import make_identity
+
+F32 = mybir.dt.float32
+BF16 = mybir.dt.bfloat16
+U32 = mybir.dt.uint32
+U8 = mybir.dt.uint8
+FP8X4 = mybir.dt.float8_e4m3fn_x4
+FP8 = mybir.dt.float8_e4m3fn
+ALU = mybir.AluOpType
+ACTF = mybir.ActivationFunctionType
+
+P = 128
+G = 8
+I = 512
+H = 512
+TOK = 1024
+D = G * H
+NT = TOK // P
+Y_SCALE = 200.0
+FLOPS = 2 * TOK * G * I * H
+
+CAST_ACT = 1664
+CAST_ACT_LAST = 704
+CONTIG = False
+HEAD_PREPS = 6
+
+
+def tile_groupedlinear_kernel(tc, x, W, b, out_0, out_1):
+    nc = tc.nc
+    xv = x.flatten_outer_dims().rearrange("(n p) d -> n p d", p=P)
+    o0v = out_0.flatten_outer_dims().rearrange("(n p) d -> n p d", p=P)
+    o1v = out_1.flatten_outer_dims().rearrange("(n p) d -> n p d", p=P)
+    wv = W.rearrange("g (c p j) i -> c p g (j i)", c=2, j=2)
+
+    with ExitStack() as ctx:
+        const = ctx.enter_context(tc.tile_pool(name="const", bufs=1))
+        rawp = ctx.enter_context(tc.tile_pool(name="rawp", bufs=7))
+        grp = ctx.enter_context(tc.tile_pool(name="grp", bufs=3))
+        xqp = ctx.enter_context(tc.tile_pool(name="xqp", bufs=5))
+        outp = ctx.enter_context(tc.tile_pool(name="outp", bufs=8))
+        o8p = ctx.enter_context(tc.tile_pool(name="o8p", bufs=4))
+        psum = ctx.enter_context(tc.psum_pool(name="psum", bufs=8))
+        ctx.enter_context(tc.manual_schedule())
+
+        raw = {}
+        loads = [("x", 0, 0), ("w", 0, 0), ("w", 0, 1), ("x", 1, 0), ("w", 1, 0), ("w", 1, 1)]
+        loads.extend([("x", t, 0) for t in range(2, NT)])
+        b_rows = const.tile([P, H], BF16, name="b_rows")
+        nc.vector.memset(b_rows[:], 0.0)
+        for key in loads:
+            if key == ("w", 0, 0):
+                nc.sync.dma_start(out=b_rows[0:G, :], in_=b)
+            t_raw = rawp.tile([P, D], BF16, tag="raw", name="raw_%s%d%d" % key)
+            if key[0] == "x":
+                nc.sync.dma_start(out=t_raw[:], in_=xv[key[1]])
+            else:
+                nc.sync.dma_start(
+                    out=t_raw[:].rearrange("p (g f) -> p g f", g=4),
+                    in_=wv[key[1]][:, key[2] * 4 : key[2] * 4 + 4, :],
+                )
+            raw[key] = t_raw
+
+        warm_in = const.tile([P, 1], F32, name="warm_in")
+        warm_out = const.tile([P, 1], F32, name="warm_out")
+        nc.vector.memset(warm_in[:], 0.0)
+        nc.scalar.activation(out=warm_out[:], in_=warm_in[:], func=ACTF.Copy, scale=Y_SCALE)
+        ident_bf = const.tile([P, P], BF16, name="ident_bf")
+        make_identity(nc, ident_bf[:])
+        ident = const.tile([P, P], F32, name="ident")
+        make_identity(nc, ident[:])
+        bias = const.tile([P, D], F32, name="bias")
+
+        def bias_bank(i):
+            hq, gh = divmod(i, 2)
+            ps = psum.tile([P, 512], F32, tag="ps", name="ps_b%d" % i)
+            for gl in range(4):
+                g = gh * 4 + gl
+                nc.tensor.matmul(
+                    out=ps[:, gl * P : (gl + 1) * P],
+                    lhsT=ident_bf[:, g : g + 1].to_broadcast([P, P]),
+                    rhs=b_rows[:, hq * P : (hq + 1) * P],
+                    start=True,
+                    stop=True,
+                )
+            dst = bias[:, hq * 1024 : (hq + 1) * 1024].rearrange("t (c e) -> t c e", e=8)
+            dst = dst[:, :, gh * 4 : gh * 4 + 4]
+            src = ps[:].rearrange("t (l c) -> t c l", l=4)
+            if gh == 0:
+                nc.scalar.copy(out=dst, in_=src)
+            else:
+                nc.vector.tensor_copy(out=dst, in_=src)
+
+        grouped_of = {}
+        codes_of = {}
+        scales_of = {}
+
+        def prep_transpose(k, vector_helps):
+            kind, a0, a1 = k
+            if kind == "x":
+                words = raw[("x", a0, 0)][:].bitcast(F32)
+                bases = [[(a1 * 4 + bk * 2 + s) * 256 for s in range(2)] for bk in range(2)]
+            else:
+                words = raw[("w", a0, a1 // 2)][:].bitcast(F32)
+                bases = [[((a1 % 2) * 2 + bk) * 512 + s * 256 for s in range(2)] for bk in range(2)]
+            grouped = grp.tile([P, 2048], BF16, tag="grouped", name="grouped_%s%d%d" % k, align_bytes=64)
+            gw = grouped[:].bitcast(F32)
+            banks = []
+            for bk in range(2):
+                ps = psum.tile([P, 512], F32, tag="ps", name="ps_t%s%d%d%d" % (kind, a0, a1, bk))
+                for s in range(2):
+                    for u in range(2):
+                        q = s * 2 + u
+                        base = bases[bk][s]
+                        if CONTIG:
+                            src_w = words[:, base + u * P : base + (u + 1) * P]
+                        else:
+                            src_w = words[:, base + u : base + 256 : 2]
+                        nc.tensor.transpose(ps[:, q * P : (q + 1) * P], src_w, ident[:])
+                banks.append(ps)
+            for bk in range(2):
+                dst = gw[:, bk * 512 : (bk + 1) * 512].rearrange("p (s r u) -> p s r u", s=2, u=2)
+                src = banks[bk][:].rearrange("p (s u r) -> p s r u", s=2, u=2)
+                if bk == 1 and vector_helps:
+                    nc.vector.tensor_copy(out=dst, in_=src)
+                else:
+                    nc.scalar.copy(out=dst, in_=src)
+            grouped_of[k] = grouped
+
+        def prep_quantize(k):
+            if k[0] == "x":
+                codes = xqp.tile([P, 512], U32, tag="xc", name="xc_%d%d" % (k[1], k[2]), align_bytes=64)
+                scales = xqp.tile([P, 512], U8, tag="xs", name="xs_%d%d" % (k[1], k[2]), align_bytes=64)
+            else:
+                codes = const.tile([P, 512], U32, name="wc_%d%d" % (k[1], k[2]), align_bytes=64)
+                scales = const.tile([P, 512], U8, name="ws_%d%d" % (k[1], k[2]), align_bytes=64)
+            nc.vector.quantize_mx(out=codes[:].bitcast(FP8X4), scales=scales[:], in_=grouped_of[k][:])
+            codes_of[k] = codes
+            scales_of[k] = scales
+
+        def product_bank(tt, hh, gh, j):
+            ps = psum.tile([P, 512], F32, tag="ps", name="ps_m%d%d%d%d" % (tt, hh, gh, j))
+            xc = codes_of[("x", tt, gh)]
+            xs = scales_of[("x", tt, gh)]
+            for gl in range(4):
+                g = gh * 4 + gl
+                wc = codes_of[("w", hh, g // 2)]
+                ws = scales_of[("w", hh, g // 2)]
+                c0 = ((g % 2) * 2 + j) * P
+                nc.tensor.matmul_mx(
+                    out=ps[:, gl * P : (gl + 1) * P],
+                    lhsT=xc[:, gl * P : (gl + 1) * P].bitcast(FP8X4),
+                    lhsT_scale=xs[:, gl * P : (gl + 1) * P],
+                    rhs=wc[:, c0 : c0 + P].bitcast(FP8X4),
+                    rhs_scale=ws[:, c0 : c0 + P],
+                    start=True,
+                    stop=True,
+                )
+            return ps
+
+        def add_bias(ps, o, hh, gh, j):
+            e0 = j * 8 + gh * 4
+            dst = o[:].rearrange("t (p e) -> t p e", e=16)[:, :, e0 : e0 + 4]
+            bv = bias[:, hh * 2048 : (hh + 1) * 2048].rearrange("t (p e) -> t p e", e=16)[:, :, e0 : e0 + 4]
+            nc.vector.tensor_tensor(out=dst, in0=ps[:].rearrange("t (l p) -> t p l", l=4), in1=bv, op=ALU.add)
+
+        units = [(0, 0), (1, 0), (0, 1), (1, 1)]
+        units.extend([(t, h) for t in range(2, NT) for h in range(2)])
+        prep_slot = {
+            0: [("x", 0, 0), ("x", 0, 1), ("w", 0, 0), ("w", 0, 1), ("w", 0, 2)],
+            1: [("w", 0, 3), ("x", 1, 0)],
+            2: [("x", 1, 1)],
+            3: [("w", 1, 0)],
+            4: [("w", 1, 1), ("w", 1, 2)],
+            5: [("w", 1, 3), ("x", 2, 0)],
+            6: [("x", 2, 1)],
+        }
+        for t in range(3, NT):
+            prep_slot[4 * t - 4] = [("x", t, 0)]
+            prep_slot[4 * t - 2] = [("x", t, 1)]
+
+        o8_of = {}
+        casts_done = {}
+        state = {"pending": None, "n_prep": 0, "vcast": None, "acast": None}
+
+        def scalar_cast():
+            o, tt, hh, ca = state["acast"]
+            nc.scalar.activation(
+                out=o8_of[tt][:, hh * 2048 : hh * 2048 + ca],
+                in_=o[:, 0:ca],
+                func=ACTF.Copy,
+                scale=Y_SCALE,
+                saturate=False,
+            )
+            state["acast"] = None
+
+        def vector_cast():
+            o, tt, hh, ca = state["vcast"]
+            nc.vector.tensor_scalar(
+                out=o8_of[tt][:, hh * 2048 + ca : (hh + 1) * 2048],
+                in0=o[:, ca:2048],
+                scalar1=Y_SCALE,
+                scalar2=None,
+                op0=ALU.mult,
+                saturate=False,
+            )
+            state["vcast"] = None
+            casts_done[tt] = casts_done.get(tt, 0) + 1
+            if tt == NT - 1:
+                cols = slice(hh * 2048, (hh + 1) * 2048)
+                nc.sync.dma_start(out=o1v[tt][:, cols], in_=o8_of[tt][:, cols].bitcast(U8))
+            elif casts_done[tt] == 2:
+                nc.sync.dma_start(out=o1v[tt], in_=o8_of[tt][:].bitcast(U8))
+
+        o_now = {}
+        for v in range(2 * len(units)):
+            n, gh = divmod(v, 2)
+            tt, hh = units[n]
+            todo = prep_slot.get(v, [])
+            for k in todo:
+                i = state["n_prep"]
+                if 1 <= i <= 4:
+                    bias_bank(2 * i - 2)
+                    bias_bank(2 * i - 1)
+                prep_transpose(k, i < HEAD_PREPS)
+                state["n_prep"] = i + 1
+                if state["pending"] is not None:
+                    prep_quantize(state["pending"])
+                state["pending"] = k
+            if len(todo) == 0 and state["pending"] is not None:
+                prep_quantize(state["pending"])
+                state["pending"] = None
+
+            if state["acast"] is not None:
+                scalar_cast()
+
+            if gh == 0:
+                o_now[0] = outp.tile([P, 2048], F32, tag="o", name="o_%d%d" % (tt, hh))
+                if tt not in o8_of:
+                    o8_of[tt] = o8p.tile([P, D], FP8, tag="o8", name="o8_%d" % tt)
+            o = o_now[0]
+            ps0 = product_bank(tt, hh, gh, 0)
+            ps1 = product_bank(tt, hh, gh, 1)
+            add_bias(ps0, o, hh, gh, 0)
+            if state["vcast"] is not None:
+                vector_cast()
+            add_bias(ps1, o, hh, gh, 1)
+            if gh == 1:
+                nc.sync.dma_start(out=o0v[tt][:, hh * 2048 : (hh + 1) * 2048], in_=o[:])
+                ca = CAST_ACT_LAST if n == len(units) - 1 else CAST_ACT
+                state["acast"] = (o, tt, hh, ca)
+                state["vcast"] = (o, tt, hh, ca)
+        scalar_cast()
+        vector_cast()

@@ -22,10 +22,10 @@ NT = TOK // P
 Y_SCALE = 200.0
 FLOPS = 2 * TOK * G * I * H
 
-CAST_ACT = 1664
+CAST_ACT = 1728
 CAST_ACT_LAST = 704
 CONTIG = False
-HEAD_PREPS = 6
+HEAD_PREPS = 3
 
 
 def tile_groupedlinear_kernel(tc, x, W, b, out_0, out_1):
@@ -46,22 +46,31 @@ def tile_groupedlinear_kernel(tc, x, W, b, out_0, out_1):
         ctx.enter_context(tc.manual_schedule())
 
         raw = {}
-        loads = [("x", 0, 0), ("w", 0, 0), ("w", 0, 1), ("x", 1, 0), ("w", 1, 0), ("w", 1, 1)]
-        loads.extend([("x", t, 0) for t in range(2, NT)])
         b_rows = const.tile([P, H], BF16, name="b_rows")
         nc.vector.memset(b_rows[:], 0.0)
-        for key in loads:
-            if key == ("w", 0, 0):
-                nc.sync.dma_start(out=b_rows[0:G, :], in_=b)
-            t_raw = rawp.tile([P, D], BF16, tag="raw", name="raw_%s%d%d" % key)
-            if key[0] == "x":
-                nc.sync.dma_start(out=t_raw[:], in_=xv[key[1]])
-            else:
-                nc.sync.dma_start(
-                    out=t_raw[:].rearrange("p (g f) -> p g f", g=4),
-                    in_=wv[key[1]][:, key[2] * 4 : key[2] * 4 + 4, :],
-                )
-            raw[key] = t_raw
+        for key in [("x", 0, 0), ("w", 0, 0), ("w", 0, 1), ("x", 1, 0), ("w", 1, 0), ("w", 1, 1)]:
+            raw[key] = rawp.tile([P, D], BF16, tag="raw", name="raw_%s%d%d" % key)
+
+        def load_x(t, c0, c1):
+            nc.sync.dma_start(out=raw[("x", t, 0)][:, c0:c1], in_=xv[t][:, c0:c1])
+
+        def load_w(c, g0, g1):
+            t_raw = raw[("w", c, g0 // 4)][:].rearrange("p (g f) -> p g f", g=4)
+            nc.sync.dma_start(out=t_raw[:, g0 % 4 : g0 % 4 + g1 - g0, :], in_=wv[c][:, g0:g1, :])
+
+        load_x(0, 0, 2048)
+        nc.sync.dma_start(out=b_rows[0:G, :], in_=b)
+        load_w(0, 0, 2)
+        load_w(0, 2, 4)
+        load_x(0, 2048, 4096)
+        load_w(0, 4, 6)
+        load_w(0, 6, 8)
+        load_x(1, 0, 4096)
+        load_w(1, 0, 4)
+        load_w(1, 4, 8)
+        for t in range(2, NT):
+            raw[("x", t, 0)] = rawp.tile([P, D], BF16, tag="raw", name="raw_x%d" % t)
+            load_x(t, 0, 4096)
 
         warm_in = const.tile([P, 1], F32, name="warm_in")
         warm_out = const.tile([P, 1], F32, name="warm_out")
@@ -169,7 +178,7 @@ def tile_groupedlinear_kernel(tc, x, W, b, out_0, out_1):
         units = [(0, 0), (1, 0), (0, 1), (1, 1)]
         units.extend([(t, h) for t in range(2, NT) for h in range(2)])
         prep_slot = {
-            0: [("x", 0, 0), ("x", 0, 1), ("w", 0, 0), ("w", 0, 1), ("w", 0, 2)],
+            0: [("x", 0, 0), ("w", 0, 0), ("w", 0, 1), ("x", 0, 1), ("w", 0, 2)],
             1: [("w", 0, 3), ("x", 1, 0)],
             2: [("x", 1, 1)],
             3: [("w", 1, 0)],

@@ -178,13 +178,12 @@ def tile_groupedlinear_kernel(tc, x, W, b, out_0, out_1):
         units = [(0, 0), (1, 0), (0, 1), (1, 1)]
         units.extend([(t, h) for t in range(2, NT) for h in range(2)])
         prep_slot = {
-            0: [("x", 0, 0), ("w", 0, 0), ("w", 0, 1), ("x", 0, 1), ("w", 0, 2)],
-            1: [("w", 0, 3), ("x", 1, 0)],
-            2: [("x", 1, 1)],
-            3: [("w", 1, 0)],
-            4: [("w", 1, 1), ("w", 1, 2)],
-            5: [("w", 1, 3), ("x", 2, 0)],
-            6: [("x", 2, 1)],
+            0: [("x", 0, 0), ("w", 0, 0), ("w", 0, 1), ("x", 0, 1), ("w", 0, 2), ("w", 0, 3)],
+            1: [("x", 1, 0), ("x", 1, 1)],
+            2: [("w", 1, 0), ("w", 1, 1)],
+            3: [("w", 1, 2)],
+            4: [("w", 1, 3), ("x", 2, 0)],
+            5: [("x", 2, 1)],
         }
         for t in range(3, NT):
             prep_slot[4 * t - 4] = [("x", t, 0)]

@@ -26,21 +26,22 @@ CAST_ACT = 1728
 CAST_ACT_LAST = 704
 CONTIG = False
 HEAD_PREPS = 3
+FINE_FROM = 6
 
 
 def tile_groupedlinear_kernel(tc, x, W, b, out_0, out_1):
     nc = tc.nc
-    xv = x.flatten_outer_dims().rearrange("(n p) d -> n p d", p=P)
-    o0v = out_0.flatten_outer_dims().rearrange("(n p) d -> n p d", p=P)
-    o1v = out_1.flatten_outer_dims().rearrange("(n p) d -> n p d", p=P)
+    xv = x.flatten_outer_dims().rearrange("(n p j) d -> n p (j d)", p=P, j=2)
+    o0v = out_0.flatten_outer_dims().rearrange("(n p j) d -> n j p d", p=P, j=2)
+    o1v = out_1.flatten_outer_dims().rearrange("(n p j) d -> n j p d", p=P, j=2)
     wv = W.rearrange("g (c p j) i -> c p g (j i)", c=2, j=2)
 
     with ExitStack() as ctx:
         const = ctx.enter_context(tc.tile_pool(name="const", bufs=1))
-        rawp = ctx.enter_context(tc.tile_pool(name="rawp", bufs=7))
+        rawp = ctx.enter_context(tc.tile_pool(name="rawp", bufs=4))
         grp = ctx.enter_context(tc.tile_pool(name="grp", bufs=3))
         xqp = ctx.enter_context(tc.tile_pool(name="xqp", bufs=5))
-        outp = ctx.enter_context(tc.tile_pool(name="outp", bufs=8))
+        outp = ctx.enter_context(tc.tile_pool(name="outp", bufs=5))
         o8p = ctx.enter_context(tc.tile_pool(name="o8p", bufs=4))
         psum = ctx.enter_context(tc.psum_pool(name="psum", bufs=8))
         ctx.enter_context(tc.manual_schedule())
@@ -48,15 +49,16 @@ def tile_groupedlinear_kernel(tc, x, W, b, out_0, out_1):
         raw = {}
         b_rows = const.tile([P, H], BF16, name="b_rows")
         nc.vector.memset(b_rows[:], 0.0)
-        for key in [("x", 0, 0), ("w", 0, 0), ("w", 0, 1), ("x", 1, 0), ("w", 1, 0), ("w", 1, 1)]:
-            raw[key] = rawp.tile([P, D], BF16, tag="raw", name="raw_%s%d%d" % key)
+        for key in [("x", 0), ("w", 0), ("w", 1), ("x", 1), ("x", 2), ("x", 3)]:
+            raw[key] = rawp.tile([P, 2 * D], BF16, tag="raw", name="raw_%s%d" % key)
 
         def load_x(t, c0, c1):
-            nc.sync.dma_start(out=raw[("x", t, 0)][:, c0:c1], in_=xv[t][:, c0:c1])
+            a = (t % 2) * D
+            nc.sync.dma_start(out=raw[("x", t // 2)][:, a + c0 : a + c1], in_=xv[t // 2][:, a + c0 : a + c1])
 
         def load_w(c, g0, g1):
-            t_raw = raw[("w", c, g0 // 4)][:].rearrange("p (g f) -> p g f", g=4)
-            nc.sync.dma_start(out=t_raw[:, g0 % 4 : g0 % 4 + g1 - g0, :], in_=wv[c][:, g0:g1, :])
+            t_raw = raw[("w", c)][:].rearrange("p (g f) -> p g f", g=G)
+            nc.sync.dma_start(out=t_raw[:, g0:g1, :], in_=wv[c][:, g0:g1, :])
 
         load_x(0, 0, 2048)
         nc.sync.dma_start(out=b_rows[0:G, :], in_=b)
@@ -68,9 +70,10 @@ def tile_groupedlinear_kernel(tc, x, W, b, out_0, out_1):
         load_x(1, 0, 4096)
         load_w(1, 0, 4)
         load_w(1, 4, 8)
-        for t in range(2, NT):
-            raw[("x", t, 0)] = rawp.tile([P, D], BF16, tag="raw", name="raw_x%d" % t)
-            load_x(t, 0, 4096)
+        load_x(2, 0, 4096)
+        load_x(3, 0, 4096)
+        for n in range(2, NT // 2):
+            nc.sync.dma_start(out=raw[("x", n)][:], in_=xv[n])
 
         warm_in = const.tile([P, 1], F32, name="warm_in")
         warm_out = const.tile([P, 1], F32, name="warm_out")
@@ -109,11 +112,11 @@ def tile_groupedlinear_kernel(tc, x, W, b, out_0, out_1):
         def prep_transpose(k, vector_helps):
             kind, a0, a1 = k
             if kind == "x":
-                words = raw[("x", a0, 0)][:].bitcast(F32)
-                bases = [[(a1 * 4 + bk * 2 + s) * 256 for s in range(2)] for bk in range(2)]
+                words = raw[("x", a0 // 2)][:].bitcast(F32)
+                bases = [[(a0 % 2) * 2048 + (a1 * 4 + bk * 2 + s) * 256 for s in range(2)] for bk in range(2)]
             else:
-                words = raw[("w", a0, a1 // 2)][:].bitcast(F32)
-                bases = [[((a1 % 2) * 2 + bk) * 512 + s * 256 for s in range(2)] for bk in range(2)]
+                words = raw[("w", a0)][:].bitcast(F32)
+                bases = [[(a1 * 2 + bk) * 512 + s * 256 for s in range(2)] for bk in range(2)]
             grouped = grp.tile([P, 2048], BF16, tag="grouped", name="grouped_%s%d%d" % k, align_bytes=64)
             gw = grouped[:].bitcast(F32)
             banks = []
@@ -171,7 +174,7 @@ def tile_groupedlinear_kernel(tc, x, W, b, out_0, out_1):
 
         def add_bias(ps, o, hh, gh, j):
             e0 = j * 8 + gh * 4
-            dst = o[:].rearrange("t (p e) -> t p e", e=16)[:, :, e0 : e0 + 4]
+            dst = o[:, hh * 2048 : (hh + 1) * 2048].rearrange("t (p e) -> t p e", e=16)[:, :, e0 : e0 + 4]
             bv = bias[:, hh * 2048 : (hh + 1) * 2048].rearrange("t (p e) -> t p e", e=16)[:, :, e0 : e0 + 4]
             nc.vector.tensor_tensor(out=dst, in0=ps[:].rearrange("t (l p) -> t p l", l=4), in1=bv, op=ALU.add)
 
@@ -197,7 +200,7 @@ def tile_groupedlinear_kernel(tc, x, W, b, out_0, out_1):
             o, tt, hh, ca = state["acast"]
             nc.scalar.activation(
                 out=o8_of[tt][:, hh * 2048 : hh * 2048 + ca],
-                in_=o[:, 0:ca],
+                in_=o[:, hh * 2048 : hh * 2048 + ca],
                 func=ACTF.Copy,
                 scale=Y_SCALE,
                 saturate=False,
@@ -208,7 +211,7 @@ def tile_groupedlinear_kernel(tc, x, W, b, out_0, out_1):
             o, tt, hh, ca = state["vcast"]
             nc.vector.tensor_scalar(
                 out=o8_of[tt][:, hh * 2048 + ca : (hh + 1) * 2048],
-                in0=o[:, ca:2048],
+                in0=o[:, hh * 2048 + ca : (hh + 1) * 2048],
                 scalar1=Y_SCALE,
                 scalar2=None,
                 op0=ALU.mult,
@@ -218,11 +221,12 @@ def tile_groupedlinear_kernel(tc, x, W, b, out_0, out_1):
             casts_done[tt] = casts_done.get(tt, 0) + 1
             if tt == NT - 1:
                 cols = slice(hh * 2048, (hh + 1) * 2048)
-                nc.sync.dma_start(out=o1v[tt][:, cols], in_=o8_of[tt][:, cols].bitcast(U8))
+                nc.sync.dma_start(out=o1v[tt // 2][tt % 2][:, cols], in_=o8_of[tt][:, cols].bitcast(U8))
             elif casts_done[tt] == 2:
-                nc.sync.dma_start(out=o1v[tt], in_=o8_of[tt][:].bitcast(U8))
+                nc.sync.dma_start(out=o1v[tt // 2][tt % 2], in_=o8_of[tt][:].bitcast(U8))
 
         o_now = {}
+        halves_done = {}
         for v in range(2 * len(units)):
             n, gh = divmod(v, 2)
             tt, hh = units[n]
@@ -244,11 +248,10 @@ def tile_groupedlinear_kernel(tc, x, W, b, out_0, out_1):
             if state["acast"] is not None:
                 scalar_cast()
 
-            if gh == 0:
-                o_now[0] = outp.tile([P, 2048], F32, tag="o", name="o_%d%d" % (tt, hh))
-                if tt not in o8_of:
-                    o8_of[tt] = o8p.tile([P, D], FP8, tag="o8", name="o8_%d" % tt)
-            o = o_now[0]
+            if tt not in o8_of:
+                o_now[tt] = outp.tile([P, D], F32, tag="o", name="o_%d" % tt)
+                o8_of[tt] = o8p.tile([P, D], FP8, tag="o8", name="o8_%d" % tt)
+            o = o_now[tt]
             ps0 = product_bank(tt, hh, gh, 0)
             ps1 = product_bank(tt, hh, gh, 1)
             add_bias(ps0, o, hh, gh, 0)
@@ -256,7 +259,11 @@ def tile_groupedlinear_kernel(tc, x, W, b, out_0, out_1):
                 vector_cast()
             add_bias(ps1, o, hh, gh, 1)
             if gh == 1:
-                nc.sync.dma_start(out=o0v[tt][:, hh * 2048 : (hh + 1) * 2048], in_=o[:])
+                halves_done[tt] = halves_done.get(tt, 0) + 1
+                if tt >= FINE_FROM:
+                    nc.sync.dma_start(out=o0v[tt // 2][tt % 2][:, hh * 2048 : (hh + 1) * 2048], in_=o[:, hh * 2048 : (hh + 1) * 2048])
+                elif halves_done[tt] == 2:
+                    nc.sync.dma_start(out=o0v[tt // 2][tt % 2], in_=o[:])
                 ca = CAST_ACT_LAST if n == len(units) - 1 else CAST_ACT
                 state["acast"] = (o, tt, hh, ca)
                 state["vcast"] = (o, tt, hh, ca)

@@ -34,7 +34,7 @@ def tile_groupedlinear_kernel(tc, x, W, b, out_0, out_1):
     xv = x.flatten_outer_dims().rearrange("(n p j) d -> n p (j d)", p=P, j=2)
     o0v = out_0.flatten_outer_dims().rearrange("(n p j) d -> n j p d", p=P, j=2)
     o1v = out_1.flatten_outer_dims().rearrange("(n p j) d -> n j p d", p=P, j=2)
-    wv = W.rearrange("g (c p j) i -> c p g (j i)", c=2, j=2)
+    wv = W.flatten_outer_dims().rearrange("(q p j) i -> q p (j i)", p=P, j=8)
 
     with ExitStack() as ctx:
         const = ctx.enter_context(tc.tile_pool(name="const", bufs=1))
@@ -56,20 +56,17 @@ def tile_groupedlinear_kernel(tc, x, W, b, out_0, out_1):
             a = (t % 2) * D
             nc.sync.dma_start(out=raw[("x", t // 2)][:, a + c0 : a + c1], in_=xv[t // 2][:, a + c0 : a + c1])
 
-        def load_w(c, g0, g1):
-            t_raw = raw[("w", c)][:].rearrange("p (g f) -> p g f", g=G)
-            nc.sync.dma_start(out=t_raw[:, g0:g1, :], in_=wv[c][:, g0:g1, :])
+        def load_w(q):
+            nc.sync.dma_start(out=raw[("w", q // 2)][:, (q % 2) * D : (q % 2 + 1) * D], in_=wv[q])
 
         load_x(0, 0, 2048)
         nc.sync.dma_start(out=b_rows[0:G, :], in_=b)
-        load_w(0, 0, 2)
-        load_w(0, 2, 4)
+        load_w(0)
+        load_w(1)
         load_x(0, 2048, 4096)
-        load_w(0, 4, 6)
-        load_w(0, 6, 8)
+        load_w(2)
+        load_w(3)
         load_x(1, 0, 4096)
-        load_w(1, 0, 4)
-        load_w(1, 4, 8)
         load_x(2, 0, 4096)
         load_x(3, 0, 4096)
         for n in range(2, NT // 2):
@@ -114,17 +111,21 @@ def tile_groupedlinear_kernel(tc, x, W, b, out_0, out_1):
             if kind == "x":
                 words = raw[("x", a0 // 2)][:].bitcast(F32)
                 bases = [[(a0 % 2) * 2048 + (a1 * 4 + bk * 2 + s) * 256 for s in range(2)] for bk in range(2)]
+                grouped = grp.tile([P, 2048], BF16, tag="grouped", name="grouped_%s%d%d" % k, align_bytes=64)
             else:
-                words = raw[("w", a0)][:].bitcast(F32)
-                bases = [[(a1 * 2 + bk) * 512 + s * 256 for s in range(2)] for bk in range(2)]
-            grouped = grp.tile([P, 2048], BF16, tag="grouped", name="grouped_%s%d%d" % k, align_bytes=64)
+                words = raw[("w", a0 // 2)][:].bitcast(F32)
+                bases = [[(a0 % 2) * 2048 + (a1 * 4 + bk * 2 + s) * 256 for s in range(2)] for bk in range(2)]
+                if a1 == 0:
+                    grouped = outp.tile([P, D], BF16, tag="o", name="grouped_w%d" % a0, align_bytes=64)
+                else:
+                    grouped = grouped_of[("w", a0, 0)]
             gw = grouped[:].bitcast(F32)
             banks = []
             for bk in range(2):
                 ps = psum.tile([P, 512], F32, tag="ps", name="ps_t%s%d%d%d" % (kind, a0, a1, bk))
                 for s in range(2):
                     for u in range(2):
-                        q = s * 2 + u
+                        q = s * 2 + u if kind == "x" else u * 2 + s
                         base = bases[bk][s]
                         if CONTIG:
                             src_w = words[:, base + u * P : base + (u + 1) * P]
@@ -133,8 +134,14 @@ def tile_groupedlinear_kernel(tc, x, W, b, out_0, out_1):
                         nc.tensor.transpose(ps[:, q * P : (q + 1) * P], src_w, ident[:])
                 banks.append(ps)
             for bk in range(2):
-                dst = gw[:, bk * 512 : (bk + 1) * 512].rearrange("p (s r u) -> p s r u", s=2, u=2)
-                src = banks[bk][:].rearrange("p (s u r) -> p s r u", s=2, u=2)
+                if kind == "x":
+                    dst = gw[:, bk * 512 : (bk + 1) * 512].rearrange("p (s r u) -> p s r u", s=2, u=2)
+                    src = banks[bk][:].rearrange("p (s u r) -> p s r u", s=2, u=2)
+                else:
+                    bank = a1 * 2 + bk
+                    dst = gw.rearrange("p (ac r) -> p ac r", ac=4)[:, :, bank * 128 : (bank + 1) * 128]
+                    dst = dst.rearrange("p ac (s m u) -> p s ac m u", s=2, u=2)
+                    src = banks[bk][:].rearrange("p (u s ac m) -> p s ac m u", u=2, s=2, ac=4)
                 if bk == 1 and vector_helps:
                     nc.vector.tensor_copy(out=dst, in_=src)
                 else:
@@ -145,9 +152,11 @@ def tile_groupedlinear_kernel(tc, x, W, b, out_0, out_1):
             if k[0] == "x":
                 codes = xqp.tile([P, 512], U32, tag="xc", name="xc_%d%d" % (k[1], k[2]), align_bytes=64)
                 scales = xqp.tile([P, 512], U8, tag="xs", name="xs_%d%d" % (k[1], k[2]), align_bytes=64)
+            elif k[2] == 0:
+                return
             else:
-                codes = const.tile([P, 512], U32, name="wc_%d%d" % (k[1], k[2]), align_bytes=64)
-                scales = const.tile([P, 512], U8, name="ws_%d%d" % (k[1], k[2]), align_bytes=64)
+                codes = const.tile([P, 1024], U32, name="wc_%d" % k[1], align_bytes=64)
+                scales = const.tile([P, 1024], U8, name="ws_%d" % k[1], align_bytes=64)
             nc.vector.quantize_mx(out=codes[:].bitcast(FP8X4), scales=scales[:], in_=grouped_of[k][:])
             codes_of[k] = codes
             scales_of[k] = scales
@@ -158,9 +167,9 @@ def tile_groupedlinear_kernel(tc, x, W, b, out_0, out_1):
             xs = scales_of[("x", tt, gh)]
             for gl in range(4):
                 g = gh * 4 + gl
-                wc = codes_of[("w", hh, g // 2)]
-                ws = scales_of[("w", hh, g // 2)]
-                c0 = ((g % 2) * 2 + j) * P
+                wc = codes_of[("w", g // 2, 1)]
+                ws = scales_of[("w", g // 2, 1)]
+                c0 = ((g % 2) * 4 + hh * 2 + j) * P
                 nc.tensor.matmul_mx(
                     out=ps[:, gl * P : (gl + 1) * P],
                     lhsT=xc[:, gl * P : (gl + 1) * P].bitcast(FP8X4),
@@ -173,22 +182,23 @@ def tile_groupedlinear_kernel(tc, x, W, b, out_0, out_1):
             return ps
 
         def add_bias(ps, o, hh, gh, j):
-            e0 = j * 8 + gh * 4
-            dst = o[:, hh * 2048 : (hh + 1) * 2048].rearrange("t (p e) -> t p e", e=16)[:, :, e0 : e0 + 4]
-            bv = bias[:, hh * 2048 : (hh + 1) * 2048].rearrange("t (p e) -> t p e", e=16)[:, :, e0 : e0 + 4]
-            nc.vector.tensor_tensor(out=dst, in0=ps[:].rearrange("t (l p) -> t p l", l=4), in1=bv, op=ALU.add)
+            def cols(t_ap):
+                v = t_ap[:, hh * 2048 : (hh + 1) * 2048].rearrange("t (m e) -> t m e", e=64)[:, :, j * 32 : (j + 1) * 32]
+                return v.rearrange("t m (jl f) -> t m jl f", f=8)[:, :, :, gh * 4 : gh * 4 + 4]
 
-        units = [(0, 0), (1, 0), (0, 1), (1, 1)]
-        units.extend([(t, h) for t in range(2, NT) for h in range(2)])
+            nc.vector.tensor_tensor(
+                out=cols(o), in0=ps[:].rearrange("t (l jl m) -> t m jl l", l=4, jl=4), in1=cols(bias), op=ALU.add
+            )
+
+        slots = [(0, 0, 0), (0, 1, 0), (0, 0, 1), (0, 1, 1)]
+        slots.extend([(t, h, e) for t in range(1, NT) for h in range(2) for e in range(2)])
         prep_slot = {
-            0: [("x", 0, 0), ("w", 0, 0), ("w", 0, 1), ("x", 0, 1), ("w", 0, 2), ("w", 0, 3)],
-            1: [("x", 1, 0), ("x", 1, 1)],
-            2: [("w", 1, 0), ("w", 1, 1)],
-            3: [("w", 1, 2)],
-            4: [("w", 1, 3), ("x", 2, 0)],
-            5: [("x", 2, 1)],
+            0: [("x", 0, 0), ("w", 0, 0), ("w", 0, 1), ("w", 1, 0), ("w", 1, 1), ("x", 0, 1)],
+            1: [("w", 2, 0), ("w", 2, 1)],
+            2: [("w", 3, 0), ("w", 3, 1), ("x", 1, 0)],
+            3: [("x", 1, 1)],
         }
-        for t in range(3, NT):
+        for t in range(2, NT):
             prep_slot[4 * t - 4] = [("x", t, 0)]
             prep_slot[4 * t - 2] = [("x", t, 1)]
 
@@ -227,9 +237,8 @@ def tile_groupedlinear_kernel(tc, x, W, b, out_0, out_1):
 
         o_now = {}
         halves_done = {}
-        for v in range(2 * len(units)):
-            n, gh = divmod(v, 2)
-            tt, hh = units[n]
+        for v in range(len(slots)):
+            tt, hh, gh = slots[v]
             todo = prep_slot.get(v, [])
             for k in todo:
                 i = state["n_prep"]
@@ -249,7 +258,7 @@ def tile_groupedlinear_kernel(tc, x, W, b, out_0, out_1):
                 scalar_cast()
 
             if tt not in o8_of:
-                o_now[tt] = outp.tile([P, D], F32, tag="o", name="o_%d" % tt)
+                o_now[tt] = outp.tile([P, D], F32, tag="o", name="o_%d" % tt, align_bytes=64)
                 o8_of[tt] = o8p.tile([P, D], FP8, tag="o8", name="o8_%d" % tt)
             o = o_now[tt]
             ps0 = product_bank(tt, hh, gh, 0)
@@ -264,7 +273,7 @@ def tile_groupedlinear_kernel(tc, x, W, b, out_0, out_1):
                     nc.sync.dma_start(out=o0v[tt // 2][tt % 2][:, hh * 2048 : (hh + 1) * 2048], in_=o[:, hh * 2048 : (hh + 1) * 2048])
                 elif halves_done[tt] == 2:
                     nc.sync.dma_start(out=o0v[tt // 2][tt % 2], in_=o[:])
-                ca = CAST_ACT_LAST if n == len(units) - 1 else CAST_ACT
+                ca = CAST_ACT_LAST if v == len(slots) - 1 else CAST_ACT
                 state["acast"] = (o, tt, hh, ca)
                 state["vcast"] = (o, tt, hh, ca)
         scalar_cast()

@@ -26,7 +26,10 @@ CAST_ACT = 1728
 CAST_ACT_LAST = 704
 CONTIG = False
 HEAD_PREPS = 3
-FINE_FROM = 6
+HEAD_TILES = 2
+HEAD = "X00 b0 b1 b2 b3 W00 W01 b4 b5 b6 b7 W10 W11 X01 S000 W20 W21 S010 W30 W31 X10 S001 X11 S011 X20 S100 Q S101 X21 S110 Q S111"
+LOADS = "x0a b w0 w1 x0b w2 w3 x1 x23 x45 x67"
+FINE_FROM = 5
 
 
 def tile_groupedlinear_kernel(tc, x, W, b, out_0, out_1):
@@ -59,18 +62,25 @@ def tile_groupedlinear_kernel(tc, x, W, b, out_0, out_1):
         def load_w(q):
             nc.sync.dma_start(out=raw[("w", q // 2)][:, (q % 2) * D : (q % 2 + 1) * D], in_=wv[q])
 
-        load_x(0, 0, 2048)
-        nc.sync.dma_start(out=b_rows[0:G, :], in_=b)
-        load_w(0)
-        load_w(1)
-        load_x(0, 2048, 4096)
-        load_w(2)
-        load_w(3)
-        load_x(1, 0, 4096)
-        load_x(2, 0, 4096)
-        load_x(3, 0, 4096)
-        for n in range(2, NT // 2):
-            nc.sync.dma_start(out=raw[("x", n)][:], in_=xv[n])
+        do_load = {
+            "x0a": lambda: load_x(0, 0, 2048),
+            "x0b": lambda: load_x(0, 2048, 4096),
+            "x1a": lambda: load_x(1, 0, 2048),
+            "x1b": lambda: load_x(1, 2048, 4096),
+            "b": lambda: nc.sync.dma_start(out=b_rows[0:G, :], in_=b),
+            "w0": lambda: load_w(0),
+            "w1": lambda: load_w(1),
+            "w2": lambda: load_w(2),
+            "w3": lambda: load_w(3),
+            "x1": lambda: load_x(1, 0, 4096),
+            "x2": lambda: load_x(2, 0, 4096),
+            "x3": lambda: load_x(3, 0, 4096),
+            "x23": lambda: nc.sync.dma_start(out=raw[("x", 1)][:], in_=xv[1]),
+            "x45": lambda: nc.sync.dma_start(out=raw[("x", 2)][:], in_=xv[2]),
+            "x67": lambda: nc.sync.dma_start(out=raw[("x", 3)][:], in_=xv[3]),
+        }
+        for name in LOADS.split():
+            do_load[name]()
 
         warm_in = const.tile([P, 1], F32, name="warm_in")
         warm_out = const.tile([P, 1], F32, name="warm_out")
@@ -115,10 +125,7 @@ def tile_groupedlinear_kernel(tc, x, W, b, out_0, out_1):
             else:
                 words = raw[("w", a0 // 2)][:].bitcast(F32)
                 bases = [[(a0 % 2) * 2048 + (a1 * 4 + bk * 2 + s) * 256 for s in range(2)] for bk in range(2)]
-                if a1 == 0:
-                    grouped = outp.tile([P, D], BF16, tag="o", name="grouped_w%d" % a0, align_bytes=64)
-                else:
-                    grouped = grouped_of[("w", a0, 0)]
+                grouped = grp.tile([P, 2048], BF16, tag="grouped", name="grouped_%s%d%d" % k, align_bytes=64)
             gw = grouped[:].bitcast(F32)
             banks = []
             for bk in range(2):
@@ -138,8 +145,7 @@ def tile_groupedlinear_kernel(tc, x, W, b, out_0, out_1):
                     dst = gw[:, bk * 512 : (bk + 1) * 512].rearrange("p (s r u) -> p s r u", s=2, u=2)
                     src = banks[bk][:].rearrange("p (s u r) -> p s r u", s=2, u=2)
                 else:
-                    bank = a1 * 2 + bk
-                    dst = gw.rearrange("p (ac r) -> p ac r", ac=4)[:, :, bank * 128 : (bank + 1) * 128]
+                    dst = gw.rearrange("p (ac r) -> p ac r", ac=4)[:, :, bk * 128 : (bk + 1) * 128]
                     dst = dst.rearrange("p ac (s m u) -> p s ac m u", s=2, u=2)
                     src = banks[bk][:].rearrange("p (u s ac m) -> p s ac m u", u=2, s=2, ac=4)
                 if bk == 1 and vector_helps:
@@ -152,11 +158,9 @@ def tile_groupedlinear_kernel(tc, x, W, b, out_0, out_1):
             if k[0] == "x":
                 codes = xqp.tile([P, 512], U32, tag="xc", name="xc_%d%d" % (k[1], k[2]), align_bytes=64)
                 scales = xqp.tile([P, 512], U8, tag="xs", name="xs_%d%d" % (k[1], k[2]), align_bytes=64)
-            elif k[2] == 0:
-                return
             else:
-                codes = const.tile([P, 1024], U32, name="wc_%d" % k[1], align_bytes=64)
-                scales = const.tile([P, 1024], U8, name="ws_%d" % k[1], align_bytes=64)
+                codes = const.tile([P, 512], U32, name="wc_%d%d" % (k[1], k[2]), align_bytes=64)
+                scales = const.tile([P, 512], U8, name="ws_%d%d" % (k[1], k[2]), align_bytes=64)
             nc.vector.quantize_mx(out=codes[:].bitcast(FP8X4), scales=scales[:], in_=grouped_of[k][:])
             codes_of[k] = codes
             scales_of[k] = scales
@@ -167,9 +171,9 @@ def tile_groupedlinear_kernel(tc, x, W, b, out_0, out_1):
             xs = scales_of[("x", tt, gh)]
             for gl in range(4):
                 g = gh * 4 + gl
-                wc = codes_of[("w", g // 2, 1)]
-                ws = scales_of[("w", g // 2, 1)]
-                c0 = ((g % 2) * 4 + hh * 2 + j) * P
+                wc = codes_of[("w", g // 2, j)]
+                ws = scales_of[("w", g // 2, j)]
+                c0 = ((g % 2) * 2 + hh) * P
                 nc.tensor.matmul_mx(
                     out=ps[:, gl * P : (gl + 1) * P],
                     lhsT=xc[:, gl * P : (gl + 1) * P].bitcast(FP8X4),
@@ -184,23 +188,36 @@ def tile_groupedlinear_kernel(tc, x, W, b, out_0, out_1):
         def add_bias(ps, o, hh, gh, j):
             def cols(t_ap):
                 v = t_ap[:, hh * 2048 : (hh + 1) * 2048].rearrange("t (m e) -> t m e", e=64)[:, :, j * 32 : (j + 1) * 32]
-                return v.rearrange("t m (jl f) -> t m jl f", f=8)[:, :, :, gh * 4 : gh * 4 + 4]
+                return v.rearrange("t m (jl f) -> t jl m f", f=8)[:, :, :, gh * 4 : gh * 4 + 4]
 
             nc.vector.tensor_tensor(
-                out=cols(o), in0=ps[:].rearrange("t (l jl m) -> t m jl l", l=4, jl=4), in1=cols(bias), op=ALU.add
+                out=cols(o), in0=ps[:].rearrange("t (l jl m) -> t jl m l", l=4, jl=4), in1=cols(bias), op=ALU.add
             )
 
-        slots = [(0, 0, 0), (0, 1, 0), (0, 0, 1), (0, 1, 1)]
-        slots.extend([(t, h, e) for t in range(1, NT) for h in range(2) for e in range(2)])
-        prep_slot = {
-            0: [("x", 0, 0), ("w", 0, 0), ("w", 0, 1), ("w", 1, 0), ("w", 1, 1), ("x", 0, 1)],
-            1: [("w", 2, 0), ("w", 2, 1)],
-            2: [("w", 3, 0), ("w", 3, 1), ("x", 1, 0)],
-            3: [("x", 1, 1)],
-        }
-        for t in range(2, NT):
-            prep_slot[4 * t - 4] = [("x", t, 0)]
-            prep_slot[4 * t - 2] = [("x", t, 1)]
+        prog = []
+        for tok in HEAD.split():
+            if tok[0] == "X":
+                prog.append(("T", ("x", int(tok[1]), int(tok[2]))))
+            elif tok[0] == "W":
+                prog.append(("T", ("w", int(tok[1]), int(tok[2]))))
+            elif tok[0] == "b":
+                prog.append(("B", int(tok[1])))
+            elif tok[0] == "Q":
+                prog.append(("Q", 0))
+            else:
+                prog.append(("S", (int(tok[1]), int(tok[2]), int(tok[3]))))
+        for t in range(HEAD_TILES, NT):
+            if t + 1 < NT:
+                prog.append(("T", ("x", t + 1, 0)))
+            prog.append(("S", (t, 0, 0)))
+            prog.append(("Q", 0))
+            prog.append(("S", (t, 0, 1)))
+            if t + 1 < NT:
+                prog.append(("T", ("x", t + 1, 1)))
+            prog.append(("S", (t, 1, 0)))
+            prog.append(("Q", 0))
+            prog.append(("S", (t, 1, 1)))
+        n_slots = len([1 for s in prog if s[0] == "S"])
 
         o8_of = {}
         casts_done = {}
@@ -237,44 +254,46 @@ def tile_groupedlinear_kernel(tc, x, W, b, out_0, out_1):
 
         o_now = {}
         halves_done = {}
-        for v in range(len(slots)):
-            tt, hh, gh = slots[v]
-            todo = prep_slot.get(v, [])
-            for k in todo:
+        gh_done = {}
+        slot_no = 0
+        for what, arg in prog:
+            if what == "B":
+                bias_bank(arg)
+            elif what == "Q":
+                if state["pending"] is not None:
+                    prep_quantize(state["pending"])
+                    state["pending"] = None
+            elif what == "T":
                 i = state["n_prep"]
-                if 1 <= i <= 4:
-                    bias_bank(2 * i - 2)
-                    bias_bank(2 * i - 1)
-                prep_transpose(k, i < HEAD_PREPS)
+                prep_transpose(arg, i < HEAD_PREPS)
                 state["n_prep"] = i + 1
                 if state["pending"] is not None:
                     prep_quantize(state["pending"])
-                state["pending"] = k
-            if len(todo) == 0 and state["pending"] is not None:
-                prep_quantize(state["pending"])
-                state["pending"] = None
-
-            if state["acast"] is not None:
-                scalar_cast()
-
-            if tt not in o8_of:
-                o_now[tt] = outp.tile([P, D], F32, tag="o", name="o_%d" % tt, align_bytes=64)
-                o8_of[tt] = o8p.tile([P, D], FP8, tag="o8", name="o8_%d" % tt)
-            o = o_now[tt]
-            ps0 = product_bank(tt, hh, gh, 0)
-            ps1 = product_bank(tt, hh, gh, 1)
-            add_bias(ps0, o, hh, gh, 0)
-            if state["vcast"] is not None:
-                vector_cast()
-            add_bias(ps1, o, hh, gh, 1)
-            if gh == 1:
-                halves_done[tt] = halves_done.get(tt, 0) + 1
-                if tt >= FINE_FROM:
-                    nc.sync.dma_start(out=o0v[tt // 2][tt % 2][:, hh * 2048 : (hh + 1) * 2048], in_=o[:, hh * 2048 : (hh + 1) * 2048])
-                elif halves_done[tt] == 2:
-                    nc.sync.dma_start(out=o0v[tt // 2][tt % 2], in_=o[:])
-                ca = CAST_ACT_LAST if v == len(slots) - 1 else CAST_ACT
-                state["acast"] = (o, tt, hh, ca)
-                state["vcast"] = (o, tt, hh, ca)
+                state["pending"] = arg
+            else:
+                tt, hh, gh = arg
+                slot_no = slot_no + 1
+                if state["acast"] is not None:
+                    scalar_cast()
+                if tt not in o8_of:
+                    o_now[tt] = outp.tile([P, D], F32, tag="o", name="o_%d" % tt, align_bytes=64)
+                    o8_of[tt] = o8p.tile([P, D], FP8, tag="o8", name="o8_%d" % tt)
+                o = o_now[tt]
+                ps0 = product_bank(tt, hh, gh, 0)
+                ps1 = product_bank(tt, hh, gh, 1)
+                add_bias(ps0, o, hh, gh, 0)
+                if state["vcast"] is not None:
+                    vector_cast()
+                add_bias(ps1, o, hh, gh, 1)
+                gh_done[(tt, hh)] = gh_done.get((tt, hh), 0) + 1
+                if gh_done[(tt, hh)] == 2:
+                    halves_done[tt] = halves_done.get(tt, 0) + 1
+                    if tt >= FINE_FROM:
+                        nc.sync.dma_start(out=o0v[tt // 2][tt % 2][:, hh * 2048 : (hh + 1) * 2048], in_=o[:, hh * 2048 : (hh + 1) * 2048])
+                    elif halves_done[tt] == 2:
+                        nc.sync.dma_start(out=o0v[tt // 2][tt % 2], in_=o[:])
+                    ca = CAST_ACT_LAST if slot_no == n_slots else CAST_ACT
+                    state["acast"] = (o, tt, hh, ca)
+                    state["vcast"] = (o, tt, hh, ca)
         scalar_cast()
         vector_cast()

@@ -29,6 +29,7 @@ HEAD_PREPS = 3
 HEAD_TILES = 2
 HEAD = "X00 b0 b1 b2 b3 W00 W01 b4 b5 b6 b7 W10 W11 X01 S000 W20 W21 S010 W30 W31 X10 S001 X11 S011 X20 S100 Q S101 X21 S110 Q S111"
 LOADS = "x0a b w0 w1 x0b w2 w3 x1 x23 x45 x67"
+WARM = 6
 FINE_FROM = 5
 
 
@@ -50,6 +51,8 @@ def tile_groupedlinear_kernel(tc, x, W, b, out_0, out_1):
         ctx.enter_context(tc.manual_schedule())
 
         raw = {}
+        zeros = const.tile([P, H], BF16, name="zeros")
+        nc.vector.memset(zeros[:], 0.0)
         b_rows = const.tile([P, H], BF16, name="b_rows")
         nc.vector.memset(b_rows[:], 0.0)
         for key in [("x", 0), ("w", 0), ("w", 1), ("x", 1), ("x", 2), ("x", 3)]:
@@ -81,6 +84,10 @@ def tile_groupedlinear_kernel(tc, x, W, b, out_0, out_1):
         }
         for name in LOADS.split():
             do_load[name]()
+
+        ps_warm = psum.tile([P, 512], F32, tag="ps", name="ps_warm")
+        for i in range(WARM):
+            nc.tensor.matmul(out=ps_warm[:], lhsT=zeros[:, 0:P], rhs=zeros[:], start=True, stop=True)
 
         warm_in = const.tile([P, 1], F32, name="warm_in")
         warm_out = const.tile([P, 1], F32, name="warm_out")

@@ -30,7 +30,7 @@ HEAD_TILES = 2
 HEAD = "X00 b0 b1 b2 b3 W00 W01 b4 b5 b6 b7 W10 W11 X01 S000 W20 W21 S010 W30 W31 X10 S001 X11 S011 X20 S100 Q S101 X21 S110 Q S111"
 LOADS = "x0a b w0 w1 x0b w2 w3 x1 x23 x45 x67"
 WARM = 6
-FINE_FROM = 5
+FINE_FROM = 3
 
 
 def tile_groupedlinear_kernel(tc, x, W, b, out_0, out_1):

@@ -56,7 +56,7 @@ def tile_groupedlinear_kernel(tc, x, W, b, out_0, out_1):
         b_rows = const.tile([P, H], BF16, name="b_rows")
         nc.vector.memset(b_rows[:], 0.0)
         for key in [("x", 0), ("w", 0), ("w", 1), ("x", 1), ("x", 2), ("x", 3)]:
-            raw[key] = rawp.tile([P, 2 * D], BF16, tag="raw", name="raw_%s%d" % key)
+            raw[key] = rawp.tile([P, 2 * D], BF16, tag="raw", name="raw_%s%d" % key, align_bytes=256)
 
         def load_x(t, c0, c1):
             a = (t % 2) * D
@@ -283,8 +283,8 @@ def tile_groupedlinear_kernel(tc, x, W, b, out_0, out_1):
                 if state["acast"] is not None:
                     scalar_cast()
                 if tt not in o8_of:
-                    o_now[tt] = outp.tile([P, D], F32, tag="o", name="o_%d" % tt, align_bytes=64)
-                    o8_of[tt] = o8p.tile([P, D], FP8, tag="o8", name="o8_%d" % tt)
+                    o_now[tt] = outp.tile([P, D], F32, tag="o", name="o_%d" % tt, align_bytes=256)
+                    o8_of[tt] = o8p.tile([P, D], FP8, tag="o8", name="o8_%d" % tt, align_bytes=256)
                 o = o_now[tt]
                 ps0 = product_bank(tt, hh, gh, 0)
                 ps1 = product_bank(tt, hh, gh, 1)

@@ -253,10 +253,7 @@ def tile_groupedlinear_kernel(tc, x, W, b, out_0, out_1):
             )
             state["vcast"] = None
             casts_done[tt] = casts_done.get(tt, 0) + 1
-            if tt == NT - 1:
-                cols = slice(hh * 2048, (hh + 1) * 2048)
-                nc.sync.dma_start(out=o1v[tt // 2][tt % 2][:, cols], in_=o8_of[tt][:, cols].bitcast(U8))
-            elif casts_done[tt] == 2:
+            if casts_done[tt] == 2:
                 nc.sync.dma_start(out=o1v[tt // 2][tt % 2], in_=o8_of[tt][:].bitcast(U8))
 
         o_now = {}

from contextlib import ExitStack

import concourse.mybir as mybir
from concourse.masks import make_identity

F32 = mybir.dt.float32
BF16 = mybir.dt.bfloat16
U32 = mybir.dt.uint32
U8 = mybir.dt.uint8
FP8X4 = mybir.dt.float8_e4m3fn_x4
FP8 = mybir.dt.float8_e4m3fn
ALU = mybir.AluOpType
ACTF = mybir.ActivationFunctionType

P = 128
G = 8
I = 512
H = 512
TOK = 1024
D = G * H
NT = TOK // P
Y_SCALE = 200.0
FLOPS = 2 * TOK * G * I * H

CAST_ACT = 1728
CAST_ACT_LAST = 704
CONTIG = False
HEAD_PREPS = 3
HEAD_TILES = 2
HEAD = "X00 b0 b1 b2 b3 W00 W01 b4 b5 b6 b7 W10 W11 X01 S000 W20 W21 S010 W30 W31 X10 S001 X11 S011 X20 S100 Q S101 X21 S110 Q S111"
LOADS = "x0a b w0 w1 x0b w2 w3 x1 x23 x45 x67"
WARM = 6
FINE_FROM = 3


def tile_groupedlinear_kernel(tc, x, W, b, out_0, out_1):
    nc = tc.nc
    xv = x.flatten_outer_dims().rearrange("(n p j) d -> n p (j d)", p=P, j=2)
    o0v = out_0.flatten_outer_dims().rearrange("(n p j) d -> n j p d", p=P, j=2)
    o1v = out_1.flatten_outer_dims().rearrange("(n p j) d -> n j p d", p=P, j=2)
    wv = W.flatten_outer_dims().rearrange("(q p j) i -> q p (j i)", p=P, j=8)

    with ExitStack() as ctx:
        const = ctx.enter_context(tc.tile_pool(name="const", bufs=1))
        rawp = ctx.enter_context(tc.tile_pool(name="rawp", bufs=4))
        grp = ctx.enter_context(tc.tile_pool(name="grp", bufs=3))
        xqp = ctx.enter_context(tc.tile_pool(name="xqp", bufs=5))
        outp = ctx.enter_context(tc.tile_pool(name="outp", bufs=5))
        o8p = ctx.enter_context(tc.tile_pool(name="o8p", bufs=4))
        psum = ctx.enter_context(tc.psum_pool(name="psum", bufs=8))
        ctx.enter_context(tc.manual_schedule())

        raw = {}
        zeros = const.tile([P, H], BF16, name="zeros")
        nc.vector.memset(zeros[:], 0.0)
        b_rows = const.tile([P, H], BF16, name="b_rows")
        nc.vector.memset(b_rows[:], 0.0)
        for key in [("x", 0), ("w", 0), ("w", 1), ("x", 1), ("x", 2), ("x", 3)]:
            raw[key] = rawp.tile([P, 2 * D], BF16, tag="raw", name="raw_%s%d" % key, align_bytes=256)

        def load_x(t, c0, c1):
            a = (t % 2) * D
            nc.sync.dma_start(out=raw[("x", t // 2)][:, a + c0 : a + c1], in_=xv[t // 2][:, a + c0 : a + c1])

        def load_w(q):
            nc.sync.dma_start(out=raw[("w", q // 2)][:, (q % 2) * D : (q % 2 + 1) * D], in_=wv[q])

        do_load = {
            "x0a": lambda: load_x(0, 0, 2048),
            "x0b": lambda: load_x(0, 2048, 4096),
            "x1a": lambda: load_x(1, 0, 2048),
            "x1b": lambda: load_x(1, 2048, 4096),
            "b": lambda: nc.sync.dma_start(out=b_rows[0:G, :], in_=b),
            "w0": lambda: load_w(0),
            "w1": lambda: load_w(1),
            "w2": lambda: load_w(2),
            "w3": lambda: load_w(3),
            "x1": lambda: load_x(1, 0, 4096),
            "x2": lambda: load_x(2, 0, 4096),
            "x3": lambda: load_x(3, 0, 4096),
            "x23": lambda: nc.sync.dma_start(out=raw[("x", 1)][:], in_=xv[1]),
            "x45": lambda: nc.sync.dma_start(out=raw[("x", 2)][:], in_=xv[2]),
            "x67": lambda: nc.sync.dma_start(out=raw[("x", 3)][:], in_=xv[3]),
        }
        for name in LOADS.split():
            do_load[name]()

        ps_warm = psum.tile([P, 512], F32, tag="ps", name="ps_warm")
        for i in range(WARM):
            nc.tensor.matmul(out=ps_warm[:], lhsT=zeros[:, 0:P], rhs=zeros[:], start=True, stop=True)

        warm_in = const.tile([P, 1], F32, name="warm_in")
        warm_out = const.tile([P, 1], F32, name="warm_out")
        nc.vector.memset(warm_in[:], 0.0)
        nc.scalar.activation(out=warm_out[:], in_=warm_in[:], func=ACTF.Copy, scale=Y_SCALE)
        ident_bf = const.tile([P, P], BF16, name="ident_bf")
        make_identity(nc, ident_bf[:])
        ident = const.tile([P, P], F32, name="ident")
        make_identity(nc, ident[:])
        bias = const.tile([P, D], F32, name="bias")

        def bias_bank(i):
            hq, gh = divmod(i, 2)
            ps = psum.tile([P, 512], F32, tag="ps", name="ps_b%d" % i)
            for gl in range(4):
                g = gh * 4 + gl
                nc.tensor.matmul(
                    out=ps[:, gl * P : (gl + 1) * P],
                    lhsT=ident_bf[:, g : g + 1].to_broadcast([P, P]),
                    rhs=b_rows[:, hq * P : (hq + 1) * P],
                    start=True,
                    stop=True,
                )
            dst = bias[:, hq * 1024 : (hq + 1) * 1024].rearrange("t (c e) -> t c e", e=8)
            dst = dst[:, :, gh * 4 : gh * 4 + 4]
            src = ps[:].rearrange("t (l c) -> t c l", l=4)
            if gh == 0:
                nc.scalar.copy(out=dst, in_=src)
            else:
                nc.vector.tensor_copy(out=dst, in_=src)

        grouped_of = {}
        codes_of = {}
        scales_of = {}

        def prep_transpose(k, vector_helps):
            kind, a0, a1 = k
            if kind == "x":
                words = raw[("x", a0 // 2)][:].bitcast(F32)
                bases = [[(a0 % 2) * 2048 + (a1 * 4 + bk * 2 + s) * 256 for s in range(2)] for bk in range(2)]
                grouped = grp.tile([P, 2048], BF16, tag="grouped", name="grouped_%s%d%d" % k, align_bytes=64)
            else:
                words = raw[("w", a0 // 2)][:].bitcast(F32)
                bases = [[(a0 % 2) * 2048 + (a1 * 4 + bk * 2 + s) * 256 for s in range(2)] for bk in range(2)]
                grouped = grp.tile([P, 2048], BF16, tag="grouped", name="grouped_%s%d%d" % k, align_bytes=64)
            gw = grouped[:].bitcast(F32)
            banks = []
            for bk in range(2):
                ps = psum.tile([P, 512], F32, tag="ps", name="ps_t%s%d%d%d" % (kind, a0, a1, bk))
                for s in range(2):
                    for u in range(2):
                        q = s * 2 + u if kind == "x" else u * 2 + s
                        base = bases[bk][s]
                        if CONTIG:
                            src_w = words[:, base + u * P : base + (u + 1) * P]
                        else:
                            src_w = words[:, base + u : base + 256 : 2]
                        nc.tensor.transpose(ps[:, q * P : (q + 1) * P], src_w, ident[:])
                banks.append(ps)
            for bk in range(2):
                if kind == "x":
                    dst = gw[:, bk * 512 : (bk + 1) * 512].rearrange("p (s r u) -> p s r u", s=2, u=2)
                    src = banks[bk][:].rearrange("p (s u r) -> p s r u", s=2, u=2)
                else:
                    dst = gw.rearrange("p (ac r) -> p ac r", ac=4)[:, :, bk * 128 : (bk + 1) * 128]
                    dst = dst.rearrange("p ac (s m u) -> p s ac m u", s=2, u=2)
                    src = banks[bk][:].rearrange("p (u s ac m) -> p s ac m u", u=2, s=2, ac=4)
                if bk == 1 and vector_helps:
                    nc.vector.tensor_copy(out=dst, in_=src)
                else:
                    nc.scalar.copy(out=dst, in_=src)
            grouped_of[k] = grouped

        def prep_quantize(k):
            if k[0] == "x":
                codes = xqp.tile([P, 512], U32, tag="xc", name="xc_%d%d" % (k[1], k[2]), align_bytes=64)
                scales = xqp.tile([P, 512], U8, tag="xs", name="xs_%d%d" % (k[1], k[2]), align_bytes=64)
            else:
                codes = const.tile([P, 512], U32, name="wc_%d%d" % (k[1], k[2]), align_bytes=64)
                scales = const.tile([P, 512], U8, name="ws_%d%d" % (k[1], k[2]), align_bytes=64)
            nc.vector.quantize_mx(out=codes[:].bitcast(FP8X4), scales=scales[:], in_=grouped_of[k][:])
            codes_of[k] = codes
            scales_of[k] = scales

        def product_bank(tt, hh, gh, j):
            ps = psum.tile([P, 512], F32, tag="ps", name="ps_m%d%d%d%d" % (tt, hh, gh, j))
            xc = codes_of[("x", tt, gh)]
            xs = scales_of[("x", tt, gh)]
            for gl in range(4):
                g = gh * 4 + gl
                wc = codes_of[("w", g // 2, j)]
                ws = scales_of[("w", g // 2, j)]
                c0 = ((g % 2) * 2 + hh) * P
                nc.tensor.matmul_mx(
                    out=ps[:, gl * P : (gl + 1) * P],
                    lhsT=xc[:, gl * P : (gl + 1) * P].bitcast(FP8X4),
                    lhsT_scale=xs[:, gl * P : (gl + 1) * P],
                    rhs=wc[:, c0 : c0 + P].bitcast(FP8X4),
                    rhs_scale=ws[:, c0 : c0 + P],
                    start=True,
                    stop=True,
                )
            return ps

        def add_bias(ps, o, hh, gh, j):
            def cols(t_ap):
                v = t_ap[:, hh * 2048 : (hh + 1) * 2048].rearrange("t (m e) -> t m e", e=64)[:, :, j * 32 : (j + 1) * 32]
                return v.rearrange("t m (jl f) -> t jl m f", f=8)[:, :, :, gh * 4 : gh * 4 + 4]

            nc.vector.tensor_tensor(
                out=cols(o), in0=ps[:].rearrange("t (l jl m) -> t jl m l", l=4, jl=4), in1=cols(bias), op=ALU.add
            )

        prog = []
        for tok in HEAD.split():
            if tok[0] == "X":
                prog.append(("T", ("x", int(tok[1]), int(tok[2]))))
            elif tok[0] == "W":
                prog.append(("T", ("w", int(tok[1]), int(tok[2]))))
            elif tok[0] == "b":
                prog.append(("B", int(tok[1])))
            elif tok[0] == "Q":
                prog.append(("Q", 0))
            else:
                prog.append(("S", (int(tok[1]), int(tok[2]), int(tok[3]))))
        for t in range(HEAD_TILES, NT):
            if t + 1 < NT:
                prog.append(("T", ("x", t + 1, 0)))
            prog.append(("S", (t, 0, 0)))
            prog.append(("Q", 0))
            prog.append(("S", (t, 0, 1)))
            if t + 1 < NT:
                prog.append(("T", ("x", t + 1, 1)))
            prog.append(("S", (t, 1, 0)))
            prog.append(("Q", 0))
            prog.append(("S", (t, 1, 1)))
        n_slots = len([1 for s in prog if s[0] == "S"])

        o8_of = {}
        casts_done = {}
        state = {"pending": None, "n_prep": 0, "vcast": None, "acast": None}

        def scalar_cast():
            o, tt, hh, ca = state["acast"]
            nc.scalar.activation(
                out=o8_of[tt][:, hh * 2048 : hh * 2048 + ca],
                in_=o[:, hh * 2048 : hh * 2048 + ca],
                func=ACTF.Copy,
                scale=Y_SCALE,
                saturate=False,
            )
            state["acast"] = None

        def vector_cast():
            o, tt, hh, ca = state["vcast"]
            nc.vector.tensor_scalar(
                out=o8_of[tt][:, hh * 2048 + ca : (hh + 1) * 2048],
                in0=o[:, hh * 2048 + ca : (hh + 1) * 2048],
                scalar1=Y_SCALE,
                scalar2=None,
                op0=ALU.mult,
                saturate=False,
            )
            state["vcast"] = None
            casts_done[tt] = casts_done.get(tt, 0) + 1
            if casts_done[tt] == 2:
                nc.sync.dma_start(out=o1v[tt // 2][tt % 2], in_=o8_of[tt][:].bitcast(U8))

        o_now = {}
        halves_done = {}
        gh_done = {}
        slot_no = 0
        for what, arg in prog:
            if what == "B":
                bias_bank(arg)
            elif what == "Q":
                if state["pending"] is not None:
                    prep_quantize(state["pending"])
                    state["pending"] = None
            elif what == "T":
                i = state["n_prep"]
                prep_transpose(arg, i < HEAD_PREPS)
                state["n_prep"] = i + 1
                if state["pending"] is not None:
                    prep_quantize(state["pending"])
                state["pending"] = arg
            else:
                tt, hh, gh = arg
                slot_no = slot_no + 1
                if state["acast"] is not None:
                    scalar_cast()
                if tt not in o8_of:
                    o_now[tt] = outp.tile([P, D], F32, tag="o", name="o_%d" % tt, align_bytes=256)
                    o8_of[tt] = o8p.tile([P, D], FP8, tag="o8", name="o8_%d" % tt, align_bytes=256)
                o = o_now[tt]
                ps0 = product_bank(tt, hh, gh, 0)
                ps1 = product_bank(tt, hh, gh, 1)
                add_bias(ps0, o, hh, gh, 0)
                if state["vcast"] is not None:
                    vector_cast()
                add_bias(ps1, o, hh, gh, 1)
                gh_done[(tt, hh)] = gh_done.get((tt, hh), 0) + 1
                if gh_done[(tt, hh)] == 2:
                    halves_done[tt] = halves_done.get(tt, 0) + 1
                    if tt >= FINE_FROM:
                        nc.sync.dma_start(out=o0v[tt // 2][tt % 2][:, hh * 2048 : (hh + 1) * 2048], in_=o[:, hh * 2048 : (hh + 1) * 2048])
                    elif halves_done[tt] == 2:
                        nc.sync.dma_start(out=o0v[tt // 2][tt % 2], in_=o[:])
                    ca = CAST_ACT_LAST if slot_no == n_slots else CAST_ACT
                    state["acast"] = (o, tt, hh, ca)
                    state["vcast"] = (o, tt, hh, ca)
        scalar_cast()
        vector_cast()
